import numpy as np
import ml_dtypes


def mxq(x, axis, fmt="e4m3"):
    dtype, down = {"e4m3": (ml_dtypes.float8_e4m3fn, 7), "e5m2": (ml_dtypes.float8_e5m2, 14)}[fmt]
    v = np.moveaxis(np.asarray(x, np.float32).astype(ml_dtypes.bfloat16).astype(np.float64), axis, -1)
    blocks = v.reshape(v.shape[:-1] + (-1, 32))
    amax = np.abs(blocks).max(-1, keepdims=True)
    byte = np.maximum(np.where(amax > 0, np.frexp(amax)[1] - 1 + 127, 0) - down, 1)
    scale = np.exp2(byte - 127.0)
    codes = (blocks / scale).astype(np.float32).astype(dtype).astype(np.float64)
    return np.moveaxis((codes * scale).reshape(v.shape), -1, axis)


WIDE = False


def mx_kscale(k):
    if not WIDE:
        return np.ones(k)
    levels = np.array([10, -10, 5, -5, 0])
    if k % 512:
        return np.exp2(np.random.permutation(np.resize(levels, k // 32))).repeat(32)
    a = np.empty((k // 512, 16))
    for p in range(k // 512):
        a[p, :8] = np.random.permutation(np.resize(levels, 8))
        for g in range(8):
            far = levels[np.abs(levels - a[p, g]) >= 10]
            a[p, g + 8] = far[np.random.randint(len(far))]
    return np.exp2(a.ravel()).repeat(32)


BF16 = ml_dtypes.bfloat16


def bf(x):
    return np.asarray(x, np.float32).astype(BF16)


def f64(x):
    return np.asarray(x).astype(np.float64)


B, T, C, H = 4, 1024, 512, 4
HD = C // H


def rotary_pos_emb(v):
    exponents = f64(np.arange(0, HD, 2)[: HD // 2] // HD)
    freqs = 1.0 / np.power(1000.0, exponents)
    theta = f64(np.arange(T))[:, None] * freqs[None, :]
    cos = np.cos(theta)[None, :, None, :]
    sin = np.sin(theta)[None, :, None, :]
    vr = v.reshape(B, T, H, HD // 2, 2)
    v0, v1 = vr[..., 0], vr[..., 1]
    out = np.stack([v0 * cos - v1 * sin, v0 * sin + v1 * cos], axis=-1)
    return out.reshape(B, T, H, HD)


def setup_inputs():
    s = mx_kscale(C)
    return {"x": bf(np.random.standard_normal((B, T, C)) * s),
            "wq": bf(np.random.standard_normal((C, C)) / np.sqrt(C) / s[None, :]),
            "wk": bf(np.random.standard_normal((C, C)) / np.sqrt(C) / s[None, :])}


def reference(x, wq, wk):
    xm = mxq(f64(x), 2, "e4m3")
    q = (xm @ mxq(f64(wq), 1, "e4m3").T).reshape(B, T, H, HD)
    k = (xm @ mxq(f64(wk), 1, "e4m3").T).reshape(B, T, H, HD)
    return rotary_pos_emb(q), rotary_pos_emb(k)

@@ -1,0 +1,256 @@
+import math
+from contextlib import ExitStack
+
+import concourse.mybir as mybir
+from concourse.masks import make_identity
+
+F32 = mybir.dt.float32
+BF16 = mybir.dt.bfloat16
+U32 = mybir.dt.uint32
+U8 = mybir.dt.uint8
+FP8X4 = mybir.dt.float8_e4m3fn_x4
+ALU = mybir.AluOpType
+ACT = mybir.ActivationFunctionType
+
+P = 128
+BATCH, SEQ, CHANNELS = 4, 1024, 512
+TOKENS = BATCH * SEQ
+PAIRS = CHANNELS // 2
+WORDS = CHANNELS // 2
+TILES_PER_GROUP = 4
+GROUP_TOKENS = P * TILES_PER_GROUP
+GROUPS = TOKENS // GROUP_TOKENS
+GROUPS_PER_SEQ = SEQ // GROUP_TOKENS
+ANGLES = GROUPS_PER_SEQ * TILES_PER_GROUP
+TILES_PER_STORE = 2
+PSUM_BANKS = 8
+BANK = 512
+REGROUP_AT = 2
+
+FLOPS = 2 * TOKENS * CHANNELS * 2 * CHANNELS
+
+ROUND_TO_WHOLE = 1.5 * 2.0**23
+TWO_PI_HIGH = round(2.0 * math.pi * 2.0**13) / 2.0**13
+TWO_PI_LOW = 2.0 * math.pi - TWO_PI_HIGH
+
+
+def half_angle_sines(nc, consts):
+    position = consts.tile([P, ANGLES], F32)
+    nc.gpsimd.iota(
+        position[:],
+        pattern=[[GROUP_TOKENS, GROUPS_PER_SEQ], [1, TILES_PER_GROUP]],
+        base=0,
+        channel_multiplier=TILES_PER_GROUP,
+        allow_small_or_imprecise_dtypes=True,
+    )
+    shifted = consts.tile([P, ANGLES], F32)
+    nc.vector.tensor_scalar(
+        out=shifted[:], in0=position[:], scalar1=1.0 / (2.0 * math.pi), scalar2=ROUND_TO_WHOLE,
+        op0=ALU.mult, op1=ALU.add,
+    )
+    turns = consts.tile([P, ANGLES], F32)
+    nc.vector.tensor_scalar(
+        out=turns[:], in0=shifted[:], scalar1=ROUND_TO_WHOLE, scalar2=None, op0=ALU.subtract
+    )
+    coarse = consts.tile([P, ANGLES], F32)
+    nc.vector.scalar_tensor_tensor(
+        out=coarse[:], in0=turns[:], scalar=-TWO_PI_HIGH, in1=position[:], op0=ALU.mult, op1=ALU.add
+    )
+    angle = consts.tile([P, ANGLES], F32)
+    nc.vector.scalar_tensor_tensor(
+        out=angle[:], in0=turns[:], scalar=-TWO_PI_LOW, in1=coarse[:], op0=ALU.mult, op1=ALU.add
+    )
+    magnitude = consts.tile([P, ANGLES], F32)
+    nc.vector.scalar_tensor_tensor(
+        out=magnitude[:], in0=angle[:], scalar=-1.0, in1=angle[:], op0=ALU.mult, op1=ALU.max
+    )
+    complement = consts.tile([P, ANGLES], F32)
+    nc.vector.tensor_scalar(
+        out=complement[:], in0=magnitude[:], scalar1=-0.5, scalar2=math.pi / 2.0,
+        op0=ALU.mult, op1=ALU.add,
+    )
+    sin_half = consts.tile([P, ANGLES], F32)
+    nc.scalar.activation(out=sin_half[:], in_=angle[:], func=ACT.Sin, scale=0.5)
+    cos_half = consts.tile([P, ANGLES], F32)
+    nc.scalar.activation(out=cos_half[:], in_=complement[:], func=ACT.Sin)
+    return sin_half, cos_half
+
+
+def double_angles(nc, consts, sin_half, cos_half):
+    sin = consts.tile([P, ANGLES], F32)
+    nc.vector.scalar_tensor_tensor(
+        out=sin[:], in0=sin_half[:], scalar=2.0, in1=cos_half[:], op0=ALU.mult, op1=ALU.mult
+    )
+    cos_less_one = consts.tile([P, ANGLES], F32)
+    nc.vector.scalar_tensor_tensor(
+        out=cos_less_one[:], in0=sin_half[:], scalar=-2.0, in1=sin_half[:], op0=ALU.mult, op1=ALU.mult
+    )
+    cos = consts.tile([P, ANGLES], F32)
+    nc.vector.tensor_scalar(
+        out=cos[:], in0=cos_less_one[:], scalar1=1.0, scalar2=None, op0=ALU.add
+    )
+    neg_cos = consts.tile([P, ANGLES], F32)
+    nc.vector.tensor_scalar(
+        out=neg_cos[:], in0=cos_less_one[:], scalar1=-1.0, scalar2=-1.0, op0=ALU.mult, op1=ALU.add
+    )
+    return cos, neg_cos, sin
+
+
+def tile_attention_pa_t_kernel(tc, x, wq, wk, out_0, out_1):
+    nc = tc.nc
+    weights = (wq, wk)
+    x_groups = x.flatten_outer_dims().rearrange(
+        "(g p r) k -> g p (r k)", p=P, r=TILES_PER_GROUP
+    )
+    out_groups = [
+        out.rearrange("b t h d -> (b t) (h d)").rearrange(
+            "(g p r) c -> g p r c", p=P, r=TILES_PER_GROUP
+        )
+        for out in (out_0, out_1)
+    ]
+
+    with ExitStack() as stack:
+        consts = stack.enter_context(tc.tile_pool(name="consts", bufs=1))
+        x_pool = stack.enter_context(tc.tile_pool(name="x_pool", bufs=GROUPS))
+        grouped_pool = stack.enter_context(tc.tile_pool(name="grouped_pool", bufs=3))
+        quantised = stack.enter_context(tc.tile_pool(name="quantised", bufs=3))
+        terms = stack.enter_context(tc.tile_pool(name="terms", bufs=4))
+        results = stack.enter_context(tc.tile_pool(name="results", bufs=8))
+        banks = stack.enter_context(tc.psum_pool(name="banks", bufs=PSUM_BANKS))
+        stack.enter_context(tc.manual_schedule())
+
+        w_raw = [consts.tile([P, 2 * 2 * CHANNELS], BF16, name="w_raw%d" % j) for j in range(2)]
+        x_raw = [x_pool.tile([P, TILES_PER_GROUP * CHANNELS], BF16, name="x_raw") for g in range(GROUPS)]
+
+        def load_weight(j):
+            nc.sync.dma_start(
+                out=w_raw[j][:].rearrange("p (h f) -> p h f", h=2),
+                in_=weights[j].rearrange("(h p e) k -> p h (e k)", h=2, p=P, e=2),
+            )
+
+        load_weight(0)
+        nc.sync.dma_start(out=x_raw[0][:], in_=x_groups[0])
+        load_weight(1)
+        for g in range(1, GROUPS):
+            nc.sync.dma_start(out=x_raw[g][:], in_=x_groups[g])
+
+        sin_half, cos_half = half_angle_sines(nc, consts)
+        identity = consts.tile([P, P], F32)
+        make_identity(nc, identity[:])
+
+        def negate_odd_rows(j):
+            odd_rows = w_raw[j][:].rearrange("p (h e k) -> p h e k", h=2, e=2)[:, :, 1, :]
+            nc.vector.tensor_scalar(
+                out=odd_rows, in0=odd_rows, scalar1=-1.0, scalar2=None, op0=ALU.mult
+            )
+
+        def transpose_words(words, starts):
+            flipped = banks.tile([P, BANK], F32, tag="bank")
+            for n, start in enumerate(starts):
+                nc.tensor.transpose(
+                    flipped[:, n * P : (n + 1) * P], words[:, start : start + 2 * P - 1 : 2], identity[:]
+                )
+            return flipped
+
+        def copy_second_bank(vector_helps, out, in_):
+            if vector_helps:
+                nc.vector.tensor_copy(out=out, in_=in_)
+            else:
+                nc.scalar.copy(out=out, in_=in_)
+
+        def regroup_weight(j, vector_helps):
+            words = w_raw[j][:].bitcast(F32)
+            grouped = grouped_pool.tile([P, 4 * CHANNELS], BF16, align_bytes=64)
+            halves = grouped[:].bitcast(F32).rearrange("p (n c u) -> p n c u", n=2, u=2)
+            even = transpose_words(words, [(2 * h + 0) * WORDS + u for u in range(2) for h in range(2)])
+            nc.scalar.copy(out=halves[:, 1, :, :], in_=even[:].rearrange("p (u c) -> p c u", u=2))
+            odd = transpose_words(words, [(2 * h + 1) * WORDS + u for u in range(2) for h in range(2)])
+            copy_second_bank(
+                vector_helps, halves[:, 0, :, :], odd[:].rearrange("p (u c) -> p c u", u=2)
+            )
+            return grouped
+
+        def regroup_tokens(g, vector_helps):
+            words = x_raw[g][:].bitcast(F32)
+            grouped = grouped_pool.tile([P, 4 * GROUP_TOKENS], BF16, align_bytes=64)
+            halves = grouped[:].bitcast(F32).rearrange("p (n r c u) -> p n r c u", n=2, r=2, u=2)
+            first = transpose_words(words, [r * WORDS + u for r in (0, 1) for u in range(2)])
+            nc.scalar.copy(
+                out=halves[:, 0, :, :, :], in_=first[:].rearrange("p (r u c) -> p r c u", r=2, u=2)
+            )
+            last = transpose_words(words, [r * WORDS + u for r in (2, 3) for u in range(2)])
+            copy_second_bank(
+                vector_helps, halves[:, 1, :, :, :], last[:].rearrange("p (r u c) -> p r c u", r=2, u=2)
+            )
+            return grouped
+
+        def quantise(pool, name, grouped):
+            codes = pool.tile([P, BANK], U32, name=name + "_codes", align_bytes=64)
+            scales = pool.tile([P, BANK], U8, name=name + "_scales", align_bytes=64)
+            nc.vector.quantize_mx(out=codes[:].bitcast(FP8X4), scales=scales[:], in_=grouped[:])
+            return codes, scales
+
+        def project_and_rotate(x_mx, w_mx, r, column, rotated):
+            token_tile = slice(r * P, (r + 1) * P)
+            product = banks.tile([P, BANK], F32, tag="bank")
+            nc.tensor.matmul_mx(
+                out=product[:],
+                lhsT=x_mx[0][:, token_tile].bitcast(FP8X4),
+                lhsT_scale=x_mx[1][:, token_tile],
+                rhs=w_mx[0][:].bitcast(FP8X4),
+                rhs_scale=w_mx[1][:],
+                start=True,
+                stop=True,
+            )
+            second = terms.tile([P, 2, PAIRS], F32)
+            nc.scalar.activation(
+                out=second[:, 0, :], in_=product[:, PAIRS:], func=ACT.Copy,
+                scale=cos[:, column : column + 1],
+            )
+            nc.scalar.activation(
+                out=second[:, 1, :], in_=product[:, :PAIRS], func=ACT.Copy,
+                scale=neg_cos[:, column : column + 1],
+            )
+            nc.vector.scalar_tensor_tensor(
+                out=rotated.rearrange("p (i e) -> p i e", e=2),
+                in0=product[:].rearrange("p (e i) -> p i e", e=2),
+                scalar=sin[:, column : column + 1],
+                in1=second[:].rearrange("p e i -> p i e"),
+                op0=ALU.mult,
+                op1=ALU.add,
+            )
+
+        cos, neg_cos, sin = double_angles(nc, consts, sin_half, cos_half)
+        negate_odd_rows(0)
+        grouped_wq = regroup_weight(0, vector_helps=True)
+        wq_mx = quantise(consts, "wq", grouped_wq)
+        negate_odd_rows(1)
+        grouped_x = regroup_tokens(0, vector_helps=False)
+        next_x_mx = quantise(quantised, "x", grouped_x)
+        grouped_wk = regroup_weight(1, vector_helps=False)
+        wk_mx = quantise(consts, "wk", grouped_wk)
+        w_mx = (wq_mx, wk_mx)
+
+        for g in range(GROUPS):
+            x_mx = next_x_mx
+            last_group = g == GROUPS - 1
+            made = 0
+            for first_tile in range(0, TILES_PER_GROUP, TILES_PER_STORE):
+                for j in range(2):
+                    rotated = results.tile([P, TILES_PER_STORE, CHANNELS], F32)
+                    for n in range(TILES_PER_STORE):
+                        r = first_tile + n
+                        if not last_group and made == REGROUP_AT:
+                            grouped_x = regroup_tokens(g + 1, vector_helps=True)
+                        if not last_group and made == REGROUP_AT + 1:
+                            next_x_mx = quantise(quantised, "x", grouped_x)
+                        column = (g % GROUPS_PER_SEQ) * TILES_PER_GROUP + r
+                        project_and_rotate(x_mx, w_mx[j], r, column, rotated[:, n, :])
+                        made += 1
+                        if last_group:
+                            nc.sync.dma_start(out=out_groups[j][g][:, r, :], in_=rotated[:, n, :])
+                    if not last_group:
+                        nc.sync.dma_start(
+                            out=out_groups[j][g][:, first_tile : first_tile + TILES_PER_STORE, :],
+                            in_=rotated[:],
+                        )

@@ -16,6 +16,7 @@ P = 128
 BATCH, SEQ, CHANNELS = 4, 1024, 512
 TOKENS = BATCH * SEQ
 PAIRS = CHANNELS // 2
+EVEN, ODD = 0, 1
 WORDS = CHANNELS // 2
 TILES_PER_GROUP = 4
 GROUP_TOKENS = P * TILES_PER_GROUP
@@ -119,78 +120,78 @@ def tile_attention_pa_t_kernel(tc, x, wq, wk, out_0, out_1):
         banks = stack.enter_context(tc.psum_pool(name="banks", bufs=PSUM_BANKS))
         stack.enter_context(tc.manual_schedule())
 
-        w_raw = [consts.tile([P, 2 * 2 * CHANNELS], BF16, name="w_raw%d" % j) for j in range(2)]
-        x_raw = [x_pool.tile([P, TILES_PER_GROUP * CHANNELS], BF16, name="x_raw") for g in range(GROUPS)]
+        w_raw = [
+            [consts.tile([P, 2 * CHANNELS], BF16, name="w_raw%d%d" % (j, e)) for e in (EVEN, ODD)]
+            for j in range(2)
+        ]
+        x_raw = [x_pool.tile([P, TILES_PER_GROUP * CHANNELS], BF16, name="x_raw") for g in range(1, GROUPS)]
+        x_first = [consts.tile([P, 2 * CHANNELS], BF16, name="x_first%d" % m) for m in range(2)]
 
         def load_weight(j):
-            nc.sync.dma_start(
-                out=w_raw[j][:].rearrange("p (h f) -> p h f", h=2),
-                in_=weights[j].rearrange("(h p e) k -> p h (e k)", h=2, p=P, e=2),
-            )
+            for e in (EVEN, ODD):
+                nc.sync.dma_start(
+                    out=w_raw[j][e][:].rearrange("p (n k) -> p n k", n=2),
+                    in_=weights[j].rearrange("(n p e) k -> e p n k", n=2, e=2)[e],
+                )
 
         load_weight(0)
-        nc.sync.dma_start(out=x_raw[0][:], in_=x_groups[0])
+        for m in range(2):
+            nc.sync.dma_start(
+                out=x_first[m][:], in_=x_groups[0][:, m * 2 * CHANNELS : (m + 1) * 2 * CHANNELS]
+            )
         load_weight(1)
         for g in range(1, GROUPS):
-            nc.sync.dma_start(out=x_raw[g][:], in_=x_groups[g])
+            nc.sync.dma_start(out=x_raw[g - 1][:], in_=x_groups[g])
 
         sin_half, cos_half = half_angle_sines(nc, consts)
         identity = consts.tile([P, P], F32)
         make_identity(nc, identity[:])
 
         def negate_odd_rows(j):
-            odd_rows = w_raw[j][:].rearrange("p (h e k) -> p h e k", h=2, e=2)[:, :, 1, :]
+            odd_rows = w_raw[j][ODD][:]
             nc.vector.tensor_scalar(
                 out=odd_rows, in0=odd_rows, scalar1=-1.0, scalar2=None, op0=ALU.mult
             )
 
-        def transpose_words(words, starts):
+        def flip(raw):
+            words = raw.bitcast(F32)
             flipped = banks.tile([P, BANK], F32, tag="bank")
-            for n, start in enumerate(starts):
-                nc.tensor.transpose(
-                    flipped[:, n * P : (n + 1) * P], words[:, start : start + 2 * P - 1 : 2], identity[:]
-                )
+            for n in range(2):
+                for u in range(2):
+                    block = 2 * n + u
+                    first = n * WORDS + u
+                    nc.tensor.transpose(
+                        flipped[:, block * P : (block + 1) * P],
+                        words[:, first : first + 2 * P - 1 : 2],
+                        identity[:],
+                    )
             return flipped
 
-        def copy_second_bank(vector_helps, out, in_):
-            if vector_helps:
-                nc.vector.tensor_copy(out=out, in_=in_)
-            else:
-                nc.scalar.copy(out=out, in_=in_)
+        def flip_tokens(g, m):
+            return flip(x_raw[g - 1][:, m * 2 * CHANNELS : (m + 1) * 2 * CHANNELS])
 
-        def regroup_weight(j, vector_helps):
-            words = w_raw[j][:].bitcast(F32)
-            grouped = grouped_pool.tile([P, 4 * CHANNELS], BF16, align_bytes=64)
-            halves = grouped[:].bitcast(F32).rearrange("p (n c u) -> p n c u", n=2, u=2)
-            even = transpose_words(words, [(2 * h + 0) * WORDS + u for u in range(2) for h in range(2)])
-            nc.scalar.copy(out=halves[:, 1, :, :], in_=even[:].rearrange("p (u c) -> p c u", u=2))
-            odd = transpose_words(words, [(2 * h + 1) * WORDS + u for u in range(2) for h in range(2)])
-            copy_second_bank(
-                vector_helps, halves[:, 0, :, :], odd[:].rearrange("p (u c) -> p c u", u=2)
+        def regroup(copy, flipped, grouped):
+            copy(
+                out=grouped.bitcast(F32).rearrange("p (n c u) -> p n c u", n=2, u=2),
+                in_=flipped[:].rearrange("p (n u c) -> p n c u", n=2, u=2),
             )
-            return grouped
 
-        def regroup_tokens(g, vector_helps):
-            words = x_raw[g][:].bitcast(F32)
-            grouped = grouped_pool.tile([P, 4 * GROUP_TOKENS], BF16, align_bytes=64)
-            halves = grouped[:].bitcast(F32).rearrange("p (n r c u) -> p n r c u", n=2, r=2, u=2)
-            first = transpose_words(words, [r * WORDS + u for r in (0, 1) for u in range(2)])
-            nc.scalar.copy(
-                out=halves[:, 0, :, :, :], in_=first[:].rearrange("p (r u c) -> p r c u", r=2, u=2)
-            )
-            last = transpose_words(words, [r * WORDS + u for r in (2, 3) for u in range(2)])
-            copy_second_bank(
-                vector_helps, halves[:, 1, :, :, :], last[:].rearrange("p (r u c) -> p r c u", r=2, u=2)
-            )
-            return grouped
-
-        def quantise(pool, name, grouped):
+        def operand(pool, name):
             codes = pool.tile([P, BANK], U32, name=name + "_codes", align_bytes=64)
             scales = pool.tile([P, BANK], U8, name=name + "_scales", align_bytes=64)
-            nc.vector.quantize_mx(out=codes[:].bitcast(FP8X4), scales=scales[:], in_=grouped[:])
             return codes, scales
 
-        def project_and_rotate(x_mx, w_mx, r, column, rotated):
+        def quantise(mx, first, grouped):
+            columns = slice(first, first + grouped.shape[1] // 4)
+            nc.vector.quantize_mx(
+                out=mx[0][:, columns].bitcast(FP8X4), scales=mx[1][:, columns], in_=grouped
+            )
+
+        def half_tile():
+            half = grouped_pool.tile([P, 2 * BANK], BF16, name="half", bufs=6, align_bytes=64)
+            return half[:]
+
+        def project(x_mx, w_mx, r):
             token_tile = slice(r * P, (r + 1) * P)
             product = banks.tile([P, BANK], F32, tag="bank")
             nc.tensor.matmul_mx(
@@ -202,6 +203,9 @@ def tile_attention_pa_t_kernel(tc, x, wq, wk, out_0, out_1):
                 start=True,
                 stop=True,
             )
+            return product
+
+        def rotate(product, column, rotated):
             second = terms.tile([P, 2, PAIRS], F32)
             nc.scalar.activation(
                 out=second[:, 0, :], in_=product[:, PAIRS:], func=ACT.Copy,
@@ -220,32 +224,62 @@ def tile_attention_pa_t_kernel(tc, x, wq, wk, out_0, out_1):
                 op1=ALU.add,
             )
 
+        def angle_column(g, r):
+            return (g % GROUPS_PER_SEQ) * TILES_PER_GROUP + r
+
         cos, neg_cos, sin = double_angles(nc, consts, sin_half, cos_half)
+        w_mx = (operand(consts, "wq"), operand(consts, "wk"))
+        next_x_mx = operand(quantised, "x")
+        flipped_q_even = flip(w_raw[0][EVEN][:])
         negate_odd_rows(0)
-        grouped_wq = regroup_weight(0, vector_helps=True)
-        wq_mx = quantise(consts, "wq", grouped_wq)
+        flipped_q_odd = flip(w_raw[0][ODD][:])
+        flipped_x0 = flip(x_first[0][:])
+        flipped_x1 = flip(x_first[1][:])
+        grouped_q_even, grouped_q_odd = half_tile(), half_tile()
+        regroup(nc.vector.tensor_copy, flipped_q_even, grouped_q_even)
+        regroup(nc.scalar.copy, flipped_q_odd, grouped_q_odd)
+        quantise(w_mx[0], PAIRS, grouped_q_even)
+        grouped_x0, grouped_x1 = half_tile(), half_tile()
+        regroup(nc.scalar.copy, flipped_x0, grouped_x0)
+        quantise(w_mx[0], 0, grouped_q_odd)
+        flipped_k_even = flip(w_raw[1][EVEN][:])
+        quantise(next_x_mx, 0, grouped_x0)
         negate_odd_rows(1)
-        grouped_x = regroup_tokens(0, vector_helps=False)
-        next_x_mx = quantise(quantised, "x", grouped_x)
-        grouped_wk = regroup_weight(1, vector_helps=False)
-        wk_mx = quantise(consts, "wk", grouped_wk)
-        w_mx = (wq_mx, wk_mx)
+        regroup(nc.scalar.copy, flipped_x1, grouped_x1)
+        first_products = [project(next_x_mx, w_mx[0], r) for r in range(TILES_PER_STORE)]
+        flipped_k_odd = flip(w_raw[1][ODD][:])
+        grouped_k_even, grouped_k_odd = half_tile(), half_tile()
+        regroup(nc.vector.tensor_copy, flipped_k_even, grouped_k_even)
+        quantise(next_x_mx, PAIRS, grouped_x1)
+        first_rotated = results.tile([P, TILES_PER_STORE, CHANNELS], F32, name="rotated")
+        rotate(first_products[0], angle_column(0, 0), first_rotated[:, 0, :])
+        regroup(nc.scalar.copy, flipped_k_odd, grouped_k_odd)
+        quantise(w_mx[1], PAIRS, grouped_k_even)
+        rotate(first_products[1], angle_column(0, 1), first_rotated[:, 1, :])
+        quantise(w_mx[1], 0, grouped_k_odd)
+        nc.sync.dma_start(out=out_groups[0][0][:, 0:TILES_PER_STORE, :], in_=first_rotated[:])
 
         for g in range(GROUPS):
             x_mx = next_x_mx
             last_group = g == GROUPS - 1
             made = 0
-            for first_tile in range(0, TILES_PER_GROUP, TILES_PER_STORE):
-                for j in range(2):
-                    rotated = results.tile([P, TILES_PER_STORE, CHANNELS], F32)
+            for j in range(2):
+                for first_tile in range(0, TILES_PER_GROUP, TILES_PER_STORE):
+                    if g == 0 and made == 0:
+                        made = TILES_PER_STORE
+                        continue
+                    rotated = results.tile([P, TILES_PER_STORE, CHANNELS], F32, name="rotated")
                     for n in range(TILES_PER_STORE):
                         r = first_tile + n
                         if not last_group and made == REGROUP_AT:
-                            grouped_x = regroup_tokens(g + 1, vector_helps=True)
+                            grouped = grouped_pool.tile([P, 4 * GROUP_TOKENS], BF16, align_bytes=64)
+                            first, last = grouped[:, : 2 * BANK], grouped[:, 2 * BANK :]
+                            regroup(nc.scalar.copy, flip_tokens(g + 1, 0), first)
+                            regroup(nc.vector.tensor_copy, flip_tokens(g + 1, 1), last)
                         if not last_group and made == REGROUP_AT + 1:
-                            next_x_mx = quantise(quantised, "x", grouped_x)
-                        column = (g % GROUPS_PER_SEQ) * TILES_PER_GROUP + r
-                        project_and_rotate(x_mx, w_mx[j], r, column, rotated[:, n, :])
+                            next_x_mx = operand(quantised, "x")
+                            quantise(next_x_mx, 0, grouped[:])
+                        rotate(project(x_mx, w_mx[j], r), angle_column(g, r), rotated[:, n, :])
                         made += 1
                         if last_group:
                             nc.sync.dma_start(out=out_groups[j][g][:, r, :], in_=rotated[:, n, :])

@@ -275,7 +275,9 @@ def tile_attention_pa_t_kernel(tc, x, wq, wk, out_0, out_1):
                             grouped = grouped_pool.tile([P, 4 * GROUP_TOKENS], BF16, align_bytes=64)
                             first, last = grouped[:, : 2 * BANK], grouped[:, 2 * BANK :]
                             regroup(nc.scalar.copy, flip_tokens(g + 1, 0), first)
-                            regroup(nc.vector.tensor_copy, flip_tokens(g + 1, 1), last)
+                            regroup(
+                                nc.vector.tensor_copy if g % 2 else nc.scalar.copy, flip_tokens(g + 1, 1), last
+                            )
                         if not last_group and made == REGROUP_AT + 1:
                             next_x_mx = operand(quantised, "x")
                             quantise(next_x_mx, 0, grouped[:])

@@ -26,7 +26,8 @@ ANGLES = GROUPS_PER_SEQ * TILES_PER_GROUP
 TILES_PER_STORE = 2
 PSUM_BANKS = 8
 BANK = 512
-REGROUP_AT = 2
+PRODUCTS_PER_GROUP = 2 * TILES_PER_GROUP
+PREPARE_AHEAD = 10
 
 FLOPS = 2 * TOKENS * CHANNELS * 2 * CHANNELS
 
@@ -115,7 +116,7 @@ def tile_attention_pa_t_kernel(tc, x, wq, wk, out_0, out_1):
         x_pool = stack.enter_context(tc.tile_pool(name="x_pool", bufs=GROUPS))
         grouped_pool = stack.enter_context(tc.tile_pool(name="grouped_pool", bufs=3))
         quantised = stack.enter_context(tc.tile_pool(name="quantised", bufs=3))
-        terms = stack.enter_context(tc.tile_pool(name="terms", bufs=4))
+        terms = stack.enter_context(tc.tile_pool(name="terms", bufs=6))
         results = stack.enter_context(tc.tile_pool(name="results", bufs=8))
         banks = stack.enter_context(tc.psum_pool(name="banks", bufs=PSUM_BANKS))
         stack.enter_context(tc.manual_schedule())
@@ -229,7 +230,7 @@ def tile_attention_pa_t_kernel(tc, x, wq, wk, out_0, out_1):
 
         cos, neg_cos, sin = double_angles(nc, consts, sin_half, cos_half)
         w_mx = (operand(consts, "wq"), operand(consts, "wk"))
-        next_x_mx = operand(quantised, "x")
+        x_mx = {0: operand(quantised, "x")}
         flipped_q_even = flip(w_raw[0][EVEN][:])
         negate_odd_rows(0)
         flipped_q_odd = flip(w_raw[0][ODD][:])
@@ -243,14 +244,14 @@ def tile_attention_pa_t_kernel(tc, x, wq, wk, out_0, out_1):
         regroup(nc.scalar.copy, flipped_x0, grouped_x0)
         quantise(w_mx[0], 0, grouped_q_odd)
         flipped_k_even = flip(w_raw[1][EVEN][:])
-        quantise(next_x_mx, 0, grouped_x0)
+        quantise(x_mx[0], 0, grouped_x0)
         negate_odd_rows(1)
         regroup(nc.scalar.copy, flipped_x1, grouped_x1)
-        first_products = [project(next_x_mx, w_mx[0], r) for r in range(TILES_PER_STORE)]
+        first_products = [project(x_mx[0], w_mx[0], r) for r in range(TILES_PER_STORE)]
         flipped_k_odd = flip(w_raw[1][ODD][:])
         grouped_k_even, grouped_k_odd = half_tile(), half_tile()
         regroup(nc.vector.tensor_copy, flipped_k_even, grouped_k_even)
-        quantise(next_x_mx, PAIRS, grouped_x1)
+        quantise(x_mx[0], PAIRS, grouped_x1)
         first_rotated = results.tile([P, TILES_PER_STORE, CHANNELS], F32, name="rotated")
         rotate(first_products[0], angle_column(0, 0), first_rotated[:, 0, :])
         regroup(nc.scalar.copy, flipped_k_odd, grouped_k_odd)
@@ -259,34 +260,29 @@ def tile_attention_pa_t_kernel(tc, x, wq, wk, out_0, out_1):
         quantise(w_mx[1], 0, grouped_k_odd)
         nc.sync.dma_start(out=out_groups[0][0][:, 0:TILES_PER_STORE, :], in_=first_rotated[:])
 
-        for g in range(GROUPS):
-            x_mx = next_x_mx
-            last_group = g == GROUPS - 1
-            made = 0
-            for j in range(2):
-                for first_tile in range(0, TILES_PER_GROUP, TILES_PER_STORE):
-                    if g == 0 and made == 0:
-                        made = TILES_PER_STORE
-                        continue
-                    rotated = results.tile([P, TILES_PER_STORE, CHANNELS], F32, name="rotated")
-                    for n in range(TILES_PER_STORE):
-                        r = first_tile + n
-                        if not last_group and made == REGROUP_AT:
-                            grouped = grouped_pool.tile([P, 4 * GROUP_TOKENS], BF16, align_bytes=64)
-                            first, last = grouped[:, : 2 * BANK], grouped[:, 2 * BANK :]
-                            regroup(nc.scalar.copy, flip_tokens(g + 1, 0), first)
-                            regroup(
-                                nc.vector.tensor_copy if g % 2 else nc.scalar.copy, flip_tokens(g + 1, 1), last
-                            )
-                        if not last_group and made == REGROUP_AT + 1:
-                            next_x_mx = operand(quantised, "x")
-                            quantise(next_x_mx, 0, grouped[:])
-                        rotate(project(x_mx, w_mx[j], r), angle_column(g, r), rotated[:, n, :])
-                        made += 1
-                        if last_group:
-                            nc.sync.dma_start(out=out_groups[j][g][:, r, :], in_=rotated[:, n, :])
-                    if not last_group:
-                        nc.sync.dma_start(
-                            out=out_groups[j][g][:, first_tile : first_tile + TILES_PER_STORE, :],
-                            in_=rotated[:],
-                        )
+        starts = {
+            max(TILES_PER_STORE, PRODUCTS_PER_GROUP * g - PREPARE_AHEAD): g for g in range(1, GROUPS)
+        }
+        for n in range(TILES_PER_STORE, GROUPS * PRODUCTS_PER_GROUP):
+            if n in starts:
+                coming = starts[n]
+                grouped = grouped_pool.tile([P, 4 * GROUP_TOKENS], BF16, align_bytes=64)
+                flipped = [flip_tokens(coming, m) for m in range(2)]
+                regroup(nc.scalar.copy, flipped[0], grouped[:, : 2 * BANK])
+            if n - 1 in starts:
+                copy = nc.scalar.copy if coming % 2 else nc.vector.tensor_copy
+                regroup(copy, flipped[1], grouped[:, 2 * BANK :])
+            if n - 2 in starts:
+                x_mx[coming] = operand(quantised, "x")
+                quantise(x_mx[coming], 0, grouped[:])
+
+            g, i = divmod(n, PRODUCTS_PER_GROUP)
+            j, r = divmod(i, TILES_PER_GROUP)
+            place = r % TILES_PER_STORE
+            if place == 0:
+                rotated = results.tile([P, TILES_PER_STORE, CHANNELS], F32, name="rotated")
+            rotate(project(x_mx[g], w_mx[j], r), angle_column(g, r), rotated[:, place, :])
+            if g == GROUPS - 1:
+                nc.sync.dma_start(out=out_groups[j][g][:, r, :], in_=rotated[:, place, :])
+            elif place == TILES_PER_STORE - 1:
+                nc.sync.dma_start(out=out_groups[j][g][:, r - place : r + 1, :], in_=rotated[:])

@@ -128,19 +128,23 @@ def tile_attention_pa_t_kernel(tc, x, wq, wk, out_0, out_1):
         x_raw = [x_pool.tile([P, TILES_PER_GROUP * CHANNELS], BF16, name="x_raw") for g in range(1, GROUPS)]
         x_first = [consts.tile([P, 2 * CHANNELS], BF16, name="x_first%d" % m) for m in range(2)]
 
-        def load_weight(j):
-            for e in (EVEN, ODD):
-                nc.sync.dma_start(
-                    out=w_raw[j][e][:].rearrange("p (n k) -> p n k", n=2),
-                    in_=weights[j].rearrange("(n p e) k -> e p n k", n=2, e=2)[e],
-                )
+        def load_weight_half(j, e):
+            nc.sync.dma_start(
+                out=w_raw[j][e][:].rearrange("p (n k) -> p n k", n=2),
+                in_=weights[j].rearrange("(n p e) k -> e p n k", n=2, e=2)[e],
+            )
 
-        load_weight(0)
-        for m in range(2):
+        def load_first_tokens(m):
             nc.sync.dma_start(
                 out=x_first[m][:], in_=x_groups[0][:, m * 2 * CHANNELS : (m + 1) * 2 * CHANNELS]
             )
-        load_weight(1)
+
+        load_weight_half(0, EVEN)
+        load_first_tokens(0)
+        load_weight_half(0, ODD)
+        load_first_tokens(1)
+        load_weight_half(1, EVEN)
+        load_weight_half(1, ODD)
         for g in range(1, GROUPS):
             nc.sync.dma_start(out=x_raw[g - 1][:], in_=x_groups[g])
 
@@ -232,32 +236,32 @@ def tile_attention_pa_t_kernel(tc, x, wq, wk, out_0, out_1):
         w_mx = (operand(consts, "wq"), operand(consts, "wk"))
         x_mx = {0: operand(quantised, "x")}
         flipped_q_even = flip(w_raw[0][EVEN][:])
+        flipped_x0 = flip(x_first[0][:])
         negate_odd_rows(0)
         flipped_q_odd = flip(w_raw[0][ODD][:])
-        flipped_x0 = flip(x_first[0][:])
         flipped_x1 = flip(x_first[1][:])
         grouped_q_even, grouped_q_odd = half_tile(), half_tile()
-        regroup(nc.vector.tensor_copy, flipped_q_even, grouped_q_even)
-        regroup(nc.scalar.copy, flipped_q_odd, grouped_q_odd)
-        quantise(w_mx[0], PAIRS, grouped_q_even)
         grouped_x0, grouped_x1 = half_tile(), half_tile()
-        regroup(nc.scalar.copy, flipped_x0, grouped_x0)
-        quantise(w_mx[0], 0, grouped_q_odd)
-        flipped_k_even = flip(w_raw[1][EVEN][:])
-        quantise(x_mx[0], 0, grouped_x0)
-        negate_odd_rows(1)
-        regroup(nc.scalar.copy, flipped_x1, grouped_x1)
-        first_products = [project(x_mx[0], w_mx[0], r) for r in range(TILES_PER_STORE)]
-        flipped_k_odd = flip(w_raw[1][ODD][:])
         grouped_k_even, grouped_k_odd = half_tile(), half_tile()
-        regroup(nc.vector.tensor_copy, flipped_k_even, grouped_k_even)
+        regroup(nc.vector.tensor_copy, flipped_q_even, grouped_q_even)
+        regroup(nc.scalar.copy, flipped_x0, grouped_x0)
+        quantise(w_mx[0], PAIRS, grouped_q_even)
+        regroup(nc.scalar.copy, flipped_q_odd, grouped_q_odd)
+        flipped_k_even = flip(w_raw[1][EVEN][:])
+        negate_odd_rows(1)
+        flipped_k_odd = flip(w_raw[1][ODD][:])
+        quantise(x_mx[0], 0, grouped_x0)
+        quantise(w_mx[0], 0, grouped_q_odd)
+        first_products = [project(x_mx[0], w_mx[0], r) for r in range(TILES_PER_STORE)]
+        regroup(nc.scalar.copy, flipped_x1, grouped_x1)
+        regroup(nc.scalar.copy, flipped_k_even, grouped_k_even)
+        regroup(nc.vector.tensor_copy, flipped_k_odd, grouped_k_odd)
         quantise(x_mx[0], PAIRS, grouped_x1)
+        quantise(w_mx[1], PAIRS, grouped_k_even)
         first_rotated = results.tile([P, TILES_PER_STORE, CHANNELS], F32, name="rotated")
         rotate(first_products[0], angle_column(0, 0), first_rotated[:, 0, :])
-        regroup(nc.scalar.copy, flipped_k_odd, grouped_k_odd)
-        quantise(w_mx[1], PAIRS, grouped_k_even)
-        rotate(first_products[1], angle_column(0, 1), first_rotated[:, 1, :])
         quantise(w_mx[1], 0, grouped_k_odd)
+        rotate(first_products[1], angle_column(0, 1), first_rotated[:, 1, :])
         nc.sync.dma_start(out=out_groups[0][0][:, 0:TILES_PER_STORE, :], in_=first_rotated[:])
 
         starts = {
@@ -270,7 +274,7 @@ def tile_attention_pa_t_kernel(tc, x, wq, wk, out_0, out_1):
                 flipped = [flip_tokens(coming, m) for m in range(2)]
                 regroup(nc.scalar.copy, flipped[0], grouped[:, : 2 * BANK])
             if n - 1 in starts:
-                copy = nc.scalar.copy if coming % 2 else nc.vector.tensor_copy
+                copy = nc.vector.tensor_copy if coming == 1 or coming % 2 == 0 else nc.scalar.copy
                 regroup(copy, flipped[1], grouped[:, 2 * BANK :])
             if n - 2 in starts:
                 x_mx[coming] = operand(quantised, "x")

@@ -16,7 +16,8 @@ P = 128
 BATCH, SEQ, CHANNELS = 4, 1024, 512
 TOKENS = BATCH * SEQ
 PAIRS = CHANNELS // 2
-EVEN, ODD = 0, 1
+HALVES = 2
+HALF_PAIRS = PAIRS // HALVES
 WORDS = CHANNELS // 2
 TILES_PER_GROUP = 4
 GROUP_TOKENS = P * TILES_PER_GROUP
@@ -122,16 +123,16 @@ def tile_attention_pa_t_kernel(tc, x, wq, wk, out_0, out_1):
         stack.enter_context(tc.manual_schedule())
 
         w_raw = [
-            [consts.tile([P, 2 * CHANNELS], BF16, name="w_raw%d%d" % (j, e)) for e in (EVEN, ODD)]
+            [consts.tile([P, 2 * CHANNELS], BF16, name="w_raw%d%d" % (j, h)) for h in range(HALVES)]
             for j in range(2)
         ]
         x_raw = [x_pool.tile([P, TILES_PER_GROUP * CHANNELS], BF16, name="x_raw") for g in range(1, GROUPS)]
         x_first = [consts.tile([P, 2 * CHANNELS], BF16, name="x_first%d" % m) for m in range(2)]
 
-        def load_weight_half(j, e):
+        def load_weight_half(j, h):
             nc.sync.dma_start(
-                out=w_raw[j][e][:].rearrange("p (n k) -> p n k", n=2),
-                in_=weights[j].rearrange("(n p e) k -> e p n k", n=2, e=2)[e],
+                out=w_raw[j][h][:],
+                in_=weights[j].rearrange("(h p e) k -> h p (e k)", h=HALVES, e=2)[h],
             )
 
         def load_first_tokens(m):
@@ -139,12 +140,12 @@ def tile_attention_pa_t_kernel(tc, x, wq, wk, out_0, out_1):
                 out=x_first[m][:], in_=x_groups[0][:, m * 2 * CHANNELS : (m + 1) * 2 * CHANNELS]
             )
 
-        load_weight_half(0, EVEN)
+        load_weight_half(0, 0)
         load_first_tokens(0)
-        load_weight_half(0, ODD)
+        load_weight_half(0, 1)
         load_first_tokens(1)
-        load_weight_half(1, EVEN)
-        load_weight_half(1, ODD)
+        load_weight_half(1, 0)
+        load_weight_half(1, 1)
         for g in range(1, GROUPS):
             nc.sync.dma_start(out=x_raw[g - 1][:], in_=x_groups[g])
 
@@ -152,18 +153,18 @@ def tile_attention_pa_t_kernel(tc, x, wq, wk, out_0, out_1):
         identity = consts.tile([P, P], F32)
         make_identity(nc, identity[:])
 
-        def negate_odd_rows(j):
-            odd_rows = w_raw[j][ODD][:]
+        def negate_odd_rows(j, h):
+            odd_rows = w_raw[j][h][:, CHANNELS:]
             nc.vector.tensor_scalar(
                 out=odd_rows, in0=odd_rows, scalar1=-1.0, scalar2=None, op0=ALU.mult
             )
 
-        def flip(raw):
+        def flip(raw, places=(0, 1)):
             words = raw.bitcast(F32)
             flipped = banks.tile([P, BANK], F32, tag="bank")
             for n in range(2):
                 for u in range(2):
-                    block = 2 * n + u
+                    block = 2 * places[n] + u
                     first = n * WORDS + u
                     nc.tensor.transpose(
                         flipped[:, block * P : (block + 1) * P],
@@ -171,6 +172,9 @@ def tile_attention_pa_t_kernel(tc, x, wq, wk, out_0, out_1):
                         identity[:],
                     )
             return flipped
+
+        def flip_weight_half(j, h):
+            return flip(w_raw[j][h][:], (1, 0))
 
         def flip_tokens(g, m):
             return flip(x_raw[g - 1][:, m * 2 * CHANNELS : (m + 1) * 2 * CHANNELS])
@@ -192,9 +196,11 @@ def tile_attention_pa_t_kernel(tc, x, wq, wk, out_0, out_1):
                 out=mx[0][:, columns].bitcast(FP8X4), scales=mx[1][:, columns], in_=grouped
             )
 
-        def half_tile():
-            half = grouped_pool.tile([P, 2 * BANK], BF16, name="half", bufs=6, align_bytes=64)
-            return half[:]
+        def quantise_weight_half(j, h):
+            for n in range(2):
+                quantise(
+                    w_mx[j], n * PAIRS + h * HALF_PAIRS, grouped_w[j][h][:, n * BANK : (n + 1) * BANK]
+                )
 
         def project(x_mx, w_mx, r):
             token_tile = slice(r * P, (r + 1) * P)
@@ -235,32 +241,41 @@ def tile_attention_pa_t_kernel(tc, x, wq, wk, out_0, out_1):
         cos, neg_cos, sin = double_angles(nc, consts, sin_half, cos_half)
         w_mx = (operand(consts, "wq"), operand(consts, "wk"))
         x_mx = {0: operand(quantised, "x")}
-        flipped_q_even = flip(w_raw[0][EVEN][:])
+        grouped_w = [
+            [
+                consts.tile([P, 2 * BANK], BF16, name="grouped_w%d%d" % (j, h), align_bytes=64)
+                for h in range(HALVES)
+            ]
+            for j in range(2)
+        ]
+        grouped_x = [
+            consts.tile([P, 2 * BANK], BF16, name="grouped_x%d" % m, align_bytes=64) for m in range(2)
+        ]
+        negate_odd_rows(0, 0)
+        flipped_q0 = flip_weight_half(0, 0)
         flipped_x0 = flip(x_first[0][:])
-        negate_odd_rows(0)
-        flipped_q_odd = flip(w_raw[0][ODD][:])
+        negate_odd_rows(0, 1)
+        regroup(nc.vector.tensor_copy, flipped_q0, grouped_w[0][0][:])
+        flipped_q1 = flip_weight_half(0, 1)
         flipped_x1 = flip(x_first[1][:])
-        grouped_q_even, grouped_q_odd = half_tile(), half_tile()
-        grouped_x0, grouped_x1 = half_tile(), half_tile()
-        grouped_k_even, grouped_k_odd = half_tile(), half_tile()
-        regroup(nc.vector.tensor_copy, flipped_q_even, grouped_q_even)
-        regroup(nc.scalar.copy, flipped_x0, grouped_x0)
-        quantise(w_mx[0], PAIRS, grouped_q_even)
-        regroup(nc.scalar.copy, flipped_q_odd, grouped_q_odd)
-        flipped_k_even = flip(w_raw[1][EVEN][:])
-        negate_odd_rows(1)
-        flipped_k_odd = flip(w_raw[1][ODD][:])
-        quantise(x_mx[0], 0, grouped_x0)
-        quantise(w_mx[0], 0, grouped_q_odd)
+        regroup(nc.scalar.copy, flipped_x0, grouped_x[0][:])
+        quantise_weight_half(0, 0)
+        regroup(nc.scalar.copy, flipped_q1, grouped_w[0][1][:])
+        negate_odd_rows(1, 0)
+        flipped_k0 = flip_weight_half(1, 0)
+        quantise(x_mx[0], 0, grouped_x[0][:])
+        negate_odd_rows(1, 1)
+        flipped_k1 = flip_weight_half(1, 1)
+        quantise_weight_half(0, 1)
         first_products = [project(x_mx[0], w_mx[0], r) for r in range(TILES_PER_STORE)]
-        regroup(nc.scalar.copy, flipped_x1, grouped_x1)
-        regroup(nc.scalar.copy, flipped_k_even, grouped_k_even)
-        regroup(nc.vector.tensor_copy, flipped_k_odd, grouped_k_odd)
-        quantise(x_mx[0], PAIRS, grouped_x1)
-        quantise(w_mx[1], PAIRS, grouped_k_even)
+        regroup(nc.scalar.copy, flipped_x1, grouped_x[1][:])
+        regroup(nc.scalar.copy, flipped_k0, grouped_w[1][0][:])
+        regroup(nc.vector.tensor_copy, flipped_k1, grouped_w[1][1][:])
+        quantise(x_mx[0], PAIRS, grouped_x[1][:])
+        quantise_weight_half(1, 0)
         first_rotated = results.tile([P, TILES_PER_STORE, CHANNELS], F32, name="rotated")
         rotate(first_products[0], angle_column(0, 0), first_rotated[:, 0, :])
-        quantise(w_mx[1], 0, grouped_k_odd)
+        quantise_weight_half(1, 1)
         rotate(first_products[1], angle_column(0, 1), first_rotated[:, 1, :])
         nc.sync.dma_start(out=out_groups[0][0][:, 0:TILES_PER_STORE, :], in_=first_rotated[:])
 
@@ -286,7 +301,5 @@ def tile_attention_pa_t_kernel(tc, x, wq, wk, out_0, out_1):
             if place == 0:
                 rotated = results.tile([P, TILES_PER_STORE, CHANNELS], F32, name="rotated")
             rotate(project(x_mx[g], w_mx[j], r), angle_column(g, r), rotated[:, place, :])
-            if g == GROUPS - 1:
-                nc.sync.dma_start(out=out_groups[j][g][:, r, :], in_=rotated[:, place, :])
-            elif place == TILES_PER_STORE - 1:
+            if place == TILES_PER_STORE - 1:
                 nc.sync.dma_start(out=out_groups[j][g][:, r - place : r + 1, :], in_=rotated[:])

@@ -28,7 +28,8 @@ TILES_PER_STORE = 2
 PSUM_BANKS = 8
 BANK = 512
 PRODUCTS_PER_GROUP = 2 * TILES_PER_GROUP
-PREPARE_AHEAD = 10
+HELPED_GROUPS = GROUPS - 1
+GPSIMD_AT = 2
 
 FLOPS = 2 * TOKENS * CHANNELS * 2 * CHANNELS
 
@@ -80,23 +81,35 @@ def half_angle_sines(nc, consts):
 
 
 def double_angles(nc, consts, sin_half, cos_half):
-    sin = consts.tile([P, ANGLES], F32)
-    nc.vector.scalar_tensor_tensor(
-        out=sin[:], in0=sin_half[:], scalar=2.0, in1=cos_half[:], op0=ALU.mult, op1=ALU.mult
-    )
-    cos_less_one = consts.tile([P, ANGLES], F32)
-    nc.vector.scalar_tensor_tensor(
-        out=cos_less_one[:], in0=sin_half[:], scalar=-2.0, in1=sin_half[:], op0=ALU.mult, op1=ALU.mult
-    )
+    sin_squared = consts.tile([P, ANGLES], F32)
+    nc.gpsimd.tensor_tensor(out=sin_squared[:], in0=sin_half[:], in1=sin_half[:], op=ALU.mult)
     cos = consts.tile([P, ANGLES], F32)
-    nc.vector.tensor_scalar(
-        out=cos[:], in0=cos_less_one[:], scalar1=1.0, scalar2=None, op0=ALU.add
+    nc.gpsimd.tensor_scalar(
+        out=cos[:], in0=sin_squared[:], scalar1=-2.0, scalar2=1.0, op0=ALU.mult, op1=ALU.add
     )
     neg_cos = consts.tile([P, ANGLES], F32)
-    nc.vector.tensor_scalar(
-        out=neg_cos[:], in0=cos_less_one[:], scalar1=-1.0, scalar2=-1.0, op0=ALU.mult, op1=ALU.add
+    nc.gpsimd.tensor_scalar(
+        out=neg_cos[:], in0=sin_squared[:], scalar1=2.0, scalar2=-1.0, op0=ALU.mult, op1=ALU.add
+    )
+    half_sin = consts.tile([P, ANGLES], F32)
+    nc.gpsimd.tensor_tensor(out=half_sin[:], in0=sin_half[:], in1=cos_half[:], op=ALU.mult)
+    sin = consts.tile([P, ANGLES], F32)
+    nc.gpsimd.tensor_scalar(
+        out=sin[:], in0=half_sin[:], scalar1=2.0, scalar2=0.0, op0=ALU.mult, op1=ALU.add
     )
     return cos, neg_cos, sin
+
+
+def tangents(nc, consts, cos, sin):
+    one_over_cos = consts.tile([P, ANGLES], F32)
+    nc.vector.reciprocal(out=one_over_cos[:], in_=cos[:])
+    tan = consts.tile([P, ANGLES], F32)
+    nc.gpsimd.tensor_tensor(out=tan[:], in0=sin[:], in1=one_over_cos[:], op=ALU.mult)
+    neg_tan = consts.tile([P, ANGLES], F32)
+    nc.gpsimd.tensor_scalar(
+        out=neg_tan[:], in0=tan[:], scalar1=-1.0, scalar2=0.0, op0=ALU.mult, op1=ALU.add
+    )
+    return tan, neg_tan
 
 
 def tile_attention_pa_t_kernel(tc, x, wq, wk, out_0, out_1):
@@ -216,8 +229,8 @@ def tile_attention_pa_t_kernel(tc, x, wq, wk, out_0, out_1):
             )
             return product
 
-        def rotate(product, column, rotated):
-            second = terms.tile([P, 2, PAIRS], F32)
+        def cosine_terms(product, column, name):
+            second = terms.tile([P, 2, PAIRS], F32, name=name)
             nc.scalar.activation(
                 out=second[:, 0, :], in_=product[:, PAIRS:], func=ACT.Copy,
                 scale=cos[:, column : column + 1],
@@ -226,6 +239,10 @@ def tile_attention_pa_t_kernel(tc, x, wq, wk, out_0, out_1):
                 out=second[:, 1, :], in_=product[:, :PAIRS], func=ACT.Copy,
                 scale=neg_cos[:, column : column + 1],
             )
+            return second
+
+        def rotate(product, column, rotated):
+            second = cosine_terms(product, column, "second")
             nc.vector.scalar_tensor_tensor(
                 out=rotated.rearrange("p (i e) -> p i e", e=2),
                 in0=product[:].rearrange("p (e i) -> p i e", e=2),
@@ -233,6 +250,21 @@ def tile_attention_pa_t_kernel(tc, x, wq, wk, out_0, out_1):
                 in1=second[:].rearrange("p e i -> p i e"),
                 op0=ALU.mult,
                 op1=ALU.add,
+            )
+
+        def rotate_on_gpsimd(product, column, rotated):
+            second = cosine_terms(product, column, "second_gpsimd")
+            first = terms.tile([P, 2, PAIRS], F32)
+            for e, factor in ((0, neg_tan), (1, tan)):
+                nc.gpsimd.tensor_scalar(
+                    out=first[:, e, :], in0=second[:, 1 - e, :], scalar1=factor[:, column : column + 1],
+                    scalar2=0.0, op0=ALU.mult, op1=ALU.add,
+                )
+            nc.gpsimd.tensor_tensor(
+                out=rotated.rearrange("p (i e) -> p i e", e=2),
+                in0=first[:].rearrange("p e i -> p i e"),
+                in1=second[:].rearrange("p e i -> p i e"),
+                op=ALU.add,
             )
 
         def angle_column(g, r):
@@ -277,29 +309,45 @@ def tile_attention_pa_t_kernel(tc, x, wq, wk, out_0, out_1):
         rotate(first_products[0], angle_column(0, 0), first_rotated[:, 0, :])
         quantise_weight_half(1, 1)
         rotate(first_products[1], angle_column(0, 1), first_rotated[:, 1, :])
+        tan, neg_tan = tangents(nc, consts, cos, sin)
         nc.sync.dma_start(out=out_groups[0][0][:, 0:TILES_PER_STORE, :], in_=first_rotated[:])
 
-        starts = {
-            max(TILES_PER_STORE, PRODUCTS_PER_GROUP * g - PREPARE_AHEAD): g for g in range(1, GROUPS)
-        }
-        for n in range(TILES_PER_STORE, GROUPS * PRODUCTS_PER_GROUP):
-            if n in starts:
-                coming = starts[n]
-                grouped = grouped_pool.tile([P, 4 * GROUP_TOKENS], BF16, align_bytes=64)
-                flipped = [flip_tokens(coming, m) for m in range(2)]
-                regroup(nc.scalar.copy, flipped[0], grouped[:, : 2 * BANK])
-            if n - 1 in starts:
-                copy = nc.vector.tensor_copy if coming == 1 or coming % 2 == 0 else nc.scalar.copy
-                regroup(copy, flipped[1], grouped[:, 2 * BANK :])
-            if n - 2 in starts:
-                x_mx[coming] = operand(quantised, "x")
-                quantise(x_mx[coming], 0, grouped[:])
+        steps = {}
+        for coming in range(1, GROUPS):
+            if coming == 1:
+                places = [(0, TILES_PER_STORE + step) for step in range(3)]
+            else:
+                places = [(coming - 2, 5), (coming - 1, 0), (coming - 1, 1)]
+            for step, at in enumerate(places):
+                steps[at] = (step, coming)
 
-            g, i = divmod(n, PRODUCTS_PER_GROUP)
-            j, r = divmod(i, TILES_PER_GROUP)
-            place = r % TILES_PER_STORE
-            if place == 0:
-                rotated = results.tile([P, TILES_PER_STORE, CHANNELS], F32, name="rotated")
-            rotate(project(x_mx[g], w_mx[j], r), angle_column(g, r), rotated[:, place, :])
-            if place == TILES_PER_STORE - 1:
-                nc.sync.dma_start(out=out_groups[j][g][:, r - place : r + 1, :], in_=rotated[:])
+        for g in range(GROUPS):
+            helped = g < HELPED_GROUPS
+            for i in range(TILES_PER_STORE if g == 0 else 0, PRODUCTS_PER_GROUP):
+                step, coming = steps.get((g, i), (None, None))
+                if step == 0:
+                    grouped = grouped_pool.tile([P, 4 * GROUP_TOKENS], BF16, align_bytes=64)
+                    flipped = [flip_tokens(coming, m) for m in range(2)]
+                    regroup(nc.scalar.copy, flipped[0], grouped[:, : 2 * BANK])
+                if step == 1:
+                    regroup(nc.vector.tensor_copy, flipped[1], grouped[:, 2 * BANK :])
+                if step == 2:
+                    x_mx[coming] = operand(quantised, "x")
+                    quantise(x_mx[coming], 0, grouped[:])
+
+                j, r = divmod(i, TILES_PER_GROUP)
+                place = r % TILES_PER_STORE
+                if helped and i == (GPSIMD_AT if g else PRODUCTS_PER_GROUP - 2):
+                    last_rotated = results.tile([P, TILES_PER_STORE, CHANNELS], F32)
+                    last_r = TILES_PER_GROUP - 1
+                    rotate_on_gpsimd(
+                        project(x_mx[g], w_mx[1], last_r), angle_column(g, last_r), last_rotated[:, 1, :]
+                    )
+                if helped and i == PRODUCTS_PER_GROUP - 2:
+                    rotated = last_rotated
+                elif place == 0:
+                    rotated = results.tile([P, TILES_PER_STORE, CHANNELS], F32, name="rotated")
+                if not (helped and i == PRODUCTS_PER_GROUP - 1):
+                    rotate(project(x_mx[g], w_mx[j], r), angle_column(g, r), rotated[:, place, :])
+                if place == TILES_PER_STORE - 1:
+                    nc.sync.dma_start(out=out_groups[j][g][:, r - place : r + 1, :], in_=rotated[:])

import math
from contextlib import ExitStack

import concourse.mybir as mybir
from concourse.masks import make_identity

F32 = mybir.dt.float32
BF16 = mybir.dt.bfloat16
U32 = mybir.dt.uint32
U8 = mybir.dt.uint8
FP8X4 = mybir.dt.float8_e4m3fn_x4
ALU = mybir.AluOpType
ACT = mybir.ActivationFunctionType

P = 128
BATCH, SEQ, CHANNELS = 4, 1024, 512
TOKENS = BATCH * SEQ
PAIRS = CHANNELS // 2
HALVES = 2
HALF_PAIRS = PAIRS // HALVES
WORDS = CHANNELS // 2
TILES_PER_GROUP = 4
GROUP_TOKENS = P * TILES_PER_GROUP
GROUPS = TOKENS // GROUP_TOKENS
GROUPS_PER_SEQ = SEQ // GROUP_TOKENS
ANGLES = GROUPS_PER_SEQ * TILES_PER_GROUP
TILES_PER_STORE = 2
PSUM_BANKS = 8
BANK = 512
PRODUCTS_PER_GROUP = 2 * TILES_PER_GROUP
HELPED_GROUPS = GROUPS - 1
GPSIMD_AT = 2

FLOPS = 2 * TOKENS * CHANNELS * 2 * CHANNELS

ROUND_TO_WHOLE = 1.5 * 2.0**23
TWO_PI_HIGH = round(2.0 * math.pi * 2.0**13) / 2.0**13
TWO_PI_LOW = 2.0 * math.pi - TWO_PI_HIGH


def half_angle_sines(nc, consts):
    position = consts.tile([P, ANGLES], F32)
    nc.gpsimd.iota(
        position[:],
        pattern=[[GROUP_TOKENS, GROUPS_PER_SEQ], [1, TILES_PER_GROUP]],
        base=0,
        channel_multiplier=TILES_PER_GROUP,
        allow_small_or_imprecise_dtypes=True,
    )
    shifted = consts.tile([P, ANGLES], F32)
    nc.vector.tensor_scalar(
        out=shifted[:], in0=position[:], scalar1=1.0 / (2.0 * math.pi), scalar2=ROUND_TO_WHOLE,
        op0=ALU.mult, op1=ALU.add,
    )
    turns = consts.tile([P, ANGLES], F32)
    nc.vector.tensor_scalar(
        out=turns[:], in0=shifted[:], scalar1=ROUND_TO_WHOLE, scalar2=None, op0=ALU.subtract
    )
    coarse = consts.tile([P, ANGLES], F32)
    nc.vector.scalar_tensor_tensor(
        out=coarse[:], in0=turns[:], scalar=-TWO_PI_HIGH, in1=position[:], op0=ALU.mult, op1=ALU.add
    )
    angle = consts.tile([P, ANGLES], F32)
    nc.vector.scalar_tensor_tensor(
        out=angle[:], in0=turns[:], scalar=-TWO_PI_LOW, in1=coarse[:], op0=ALU.mult, op1=ALU.add
    )
    magnitude = consts.tile([P, ANGLES], F32)
    nc.vector.scalar_tensor_tensor(
        out=magnitude[:], in0=angle[:], scalar=-1.0, in1=angle[:], op0=ALU.mult, op1=ALU.max
    )
    complement = consts.tile([P, ANGLES], F32)
    nc.vector.tensor_scalar(
        out=complement[:], in0=magnitude[:], scalar1=-0.5, scalar2=math.pi / 2.0,
        op0=ALU.mult, op1=ALU.add,
    )
    sin_half = consts.tile([P, ANGLES], F32)
    nc.scalar.activation(out=sin_half[:], in_=angle[:], func=ACT.Sin, scale=0.5)
    cos_half = consts.tile([P, ANGLES], F32)
    nc.scalar.activation(out=cos_half[:], in_=complement[:], func=ACT.Sin)
    return sin_half, cos_half


def double_angles(nc, consts, sin_half, cos_half):
    sin_squared = consts.tile([P, ANGLES], F32)
    nc.gpsimd.tensor_tensor(out=sin_squared[:], in0=sin_half[:], in1=sin_half[:], op=ALU.mult)
    cos = consts.tile([P, ANGLES], F32)
    nc.gpsimd.tensor_scalar(
        out=cos[:], in0=sin_squared[:], scalar1=-2.0, scalar2=1.0, op0=ALU.mult, op1=ALU.add
    )
    neg_cos = consts.tile([P, ANGLES], F32)
    nc.gpsimd.tensor_scalar(
        out=neg_cos[:], in0=sin_squared[:], scalar1=2.0, scalar2=-1.0, op0=ALU.mult, op1=ALU.add
    )
    half_sin = consts.tile([P, ANGLES], F32)
    nc.gpsimd.tensor_tensor(out=half_sin[:], in0=sin_half[:], in1=cos_half[:], op=ALU.mult)
    sin = consts.tile([P, ANGLES], F32)
    nc.gpsimd.tensor_scalar(
        out=sin[:], in0=half_sin[:], scalar1=2.0, scalar2=0.0, op0=ALU.mult, op1=ALU.add
    )
    return cos, neg_cos, sin


def tangents(nc, consts, cos, sin):
    one_over_cos = consts.tile([P, ANGLES], F32)
    nc.vector.reciprocal(out=one_over_cos[:], in_=cos[:])
    tan = consts.tile([P, ANGLES], F32)
    nc.gpsimd.tensor_tensor(out=tan[:], in0=sin[:], in1=one_over_cos[:], op=ALU.mult)
    neg_tan = consts.tile([P, ANGLES], F32)
    nc.gpsimd.tensor_scalar(
        out=neg_tan[:], in0=tan[:], scalar1=-1.0, scalar2=0.0, op0=ALU.mult, op1=ALU.add
    )
    return tan, neg_tan


def tile_attention_pa_t_kernel(tc, x, wq, wk, out_0, out_1):
    nc = tc.nc
    weights = (wq, wk)
    x_groups = x.flatten_outer_dims().rearrange(
        "(g p r) k -> g p (r k)", p=P, r=TILES_PER_GROUP
    )
    out_groups = [
        out.rearrange("b t h d -> (b t) (h d)").rearrange(
            "(g p r) c -> g p r c", p=P, r=TILES_PER_GROUP
        )
        for out in (out_0, out_1)
    ]

    with ExitStack() as stack:
        consts = stack.enter_context(tc.tile_pool(name="consts", bufs=1))
        x_pool = stack.enter_context(tc.tile_pool(name="x_pool", bufs=GROUPS))
        grouped_pool = stack.enter_context(tc.tile_pool(name="grouped_pool", bufs=3))
        quantised = stack.enter_context(tc.tile_pool(name="quantised", bufs=3))
        terms = stack.enter_context(tc.tile_pool(name="terms", bufs=6))
        results = stack.enter_context(tc.tile_pool(name="results", bufs=8))
        banks = stack.enter_context(tc.psum_pool(name="banks", bufs=PSUM_BANKS))
        stack.enter_context(tc.manual_schedule())

        w_raw = [
            [consts.tile([P, 2 * CHANNELS], BF16, name="w_raw%d%d" % (j, h)) for h in range(HALVES)]
            for j in range(2)
        ]
        x_raw = [x_pool.tile([P, TILES_PER_GROUP * CHANNELS], BF16, name="x_raw") for g in range(1, GROUPS)]
        x_first = [consts.tile([P, 2 * CHANNELS], BF16, name="x_first%d" % m) for m in range(2)]

        def load_weight_half(j, h):
            nc.sync.dma_start(
                out=w_raw[j][h][:],
                in_=weights[j].rearrange("(h p e) k -> h p (e k)", h=HALVES, e=2)[h],
            )

        def load_first_tokens(m):
            nc.sync.dma_start(
                out=x_first[m][:], in_=x_groups[0][:, m * 2 * CHANNELS : (m + 1) * 2 * CHANNELS]
            )

        load_weight_half(0, 0)
        load_first_tokens(0)
        load_weight_half(0, 1)
        load_first_tokens(1)
        load_weight_half(1, 0)
        load_weight_half(1, 1)
        for g in range(1, GROUPS):
            nc.sync.dma_start(out=x_raw[g - 1][:], in_=x_groups[g])

        sin_half, cos_half = half_angle_sines(nc, consts)
        identity = consts.tile([P, P], F32)
        make_identity(nc, identity[:])

        def negate_odd_rows(j, h):
            odd_rows = w_raw[j][h][:, CHANNELS:]
            nc.vector.tensor_scalar(
                out=odd_rows, in0=odd_rows, scalar1=-1.0, scalar2=None, op0=ALU.mult
            )

        def flip(raw, places=(0, 1)):
            words = raw.bitcast(F32)
            flipped = banks.tile([P, BANK], F32, tag="bank")
            for n in range(2):
                for u in range(2):
                    block = 2 * places[n] + u
                    first = n * WORDS + u
                    nc.tensor.transpose(
                        flipped[:, block * P : (block + 1) * P],
                        words[:, first : first + 2 * P - 1 : 2],
                        identity[:],
                    )
            return flipped

        def flip_weight_half(j, h):
            return flip(w_raw[j][h][:], (1, 0))

        def flip_tokens(g, m):
            return flip(x_raw[g - 1][:, m * 2 * CHANNELS : (m + 1) * 2 * CHANNELS])

        def regroup(copy, flipped, grouped):
            copy(
                out=grouped.bitcast(F32).rearrange("p (n c u) -> p n c u", n=2, u=2),
                in_=flipped[:].rearrange("p (n u c) -> p n c u", n=2, u=2),
            )

        def operand(pool, name):
            codes = pool.tile([P, BANK], U32, name=name + "_codes", align_bytes=64)
            scales = pool.tile([P, BANK], U8, name=name + "_scales", align_bytes=64)
            return codes, scales

        def quantise(mx, first, grouped):
            columns = slice(first, first + grouped.shape[1] // 4)
            nc.vector.quantize_mx(
                out=mx[0][:, columns].bitcast(FP8X4), scales=mx[1][:, columns], in_=grouped
            )

        def quantise_weight_half(j, h):
            for n in range(2):
                quantise(
                    w_mx[j], n * PAIRS + h * HALF_PAIRS, grouped_w[j][h][:, n * BANK : (n + 1) * BANK]
                )

        def project(x_mx, w_mx, r):
            token_tile = slice(r * P, (r + 1) * P)
            product = banks.tile([P, BANK], F32, tag="bank")
            nc.tensor.matmul_mx(
                out=product[:],
                lhsT=x_mx[0][:, token_tile].bitcast(FP8X4),
                lhsT_scale=x_mx[1][:, token_tile],
                rhs=w_mx[0][:].bitcast(FP8X4),
                rhs_scale=w_mx[1][:],
                start=True,
                stop=True,
            )
            return product

        def cosine_terms(product, column, name):
            second = terms.tile([P, 2, PAIRS], F32, name=name)
            nc.scalar.activation(
                out=second[:, 0, :], in_=product[:, PAIRS:], func=ACT.Copy,
                scale=cos[:, column : column + 1],
            )
            nc.scalar.activation(
                out=second[:, 1, :], in_=product[:, :PAIRS], func=ACT.Copy,
                scale=neg_cos[:, column : column + 1],
            )
            return second

        def rotate(product, column, rotated):
            second = cosine_terms(product, column, "second")
            nc.vector.scalar_tensor_tensor(
                out=rotated.rearrange("p (i e) -> p i e", e=2),
                in0=product[:].rearrange("p (e i) -> p i e", e=2),
                scalar=sin[:, column : column + 1],
                in1=second[:].rearrange("p e i -> p i e"),
                op0=ALU.mult,
                op1=ALU.add,
            )

        def rotate_on_gpsimd(product, column, rotated):
            second = cosine_terms(product, column, "second_gpsimd")
            first = terms.tile([P, 2, PAIRS], F32)
            for e, factor in ((0, neg_tan), (1, tan)):
                nc.gpsimd.tensor_scalar(
                    out=first[:, e, :], in0=second[:, 1 - e, :], scalar1=factor[:, column : column + 1],
                    scalar2=0.0, op0=ALU.mult, op1=ALU.add,
                )
            nc.gpsimd.tensor_tensor(
                out=rotated.rearrange("p (i e) -> p i e", e=2),
                in0=first[:].rearrange("p e i -> p i e"),
                in1=second[:].rearrange("p e i -> p i e"),
                op=ALU.add,
            )

        def angle_column(g, r):
            return (g % GROUPS_PER_SEQ) * TILES_PER_GROUP + r

        cos, neg_cos, sin = double_angles(nc, consts, sin_half, cos_half)
        w_mx = (operand(consts, "wq"), operand(consts, "wk"))
        x_mx = {0: operand(quantised, "x")}
        grouped_w = [
            [
                consts.tile([P, 2 * BANK], BF16, name="grouped_w%d%d" % (j, h), align_bytes=64)
                for h in range(HALVES)
            ]
            for j in range(2)
        ]
        grouped_x = [
            consts.tile([P, 2 * BANK], BF16, name="grouped_x%d" % m, align_bytes=64) for m in range(2)
        ]
        negate_odd_rows(0, 0)
        flipped_q0 = flip_weight_half(0, 0)
        flipped_x0 = flip(x_first[0][:])
        negate_odd_rows(0, 1)
        regroup(nc.vector.tensor_copy, flipped_q0, grouped_w[0][0][:])
        flipped_q1 = flip_weight_half(0, 1)
        flipped_x1 = flip(x_first[1][:])
        regroup(nc.scalar.copy, flipped_x0, grouped_x[0][:])
        quantise_weight_half(0, 0)
        regroup(nc.scalar.copy, flipped_q1, grouped_w[0][1][:])
        negate_odd_rows(1, 0)
        flipped_k0 = flip_weight_half(1, 0)
        quantise(x_mx[0], 0, grouped_x[0][:])
        negate_odd_rows(1, 1)
        flipped_k1 = flip_weight_half(1, 1)
        quantise_weight_half(0, 1)
        first_products = [project(x_mx[0], w_mx[0], r) for r in range(TILES_PER_STORE)]
        regroup(nc.scalar.copy, flipped_x1, grouped_x[1][:])
        regroup(nc.scalar.copy, flipped_k0, grouped_w[1][0][:])
        regroup(nc.vector.tensor_copy, flipped_k1, grouped_w[1][1][:])
        quantise(x_mx[0], PAIRS, grouped_x[1][:])
        quantise_weight_half(1, 0)
        first_rotated = results.tile([P, TILES_PER_STORE, CHANNELS], F32, name="rotated")
        rotate(first_products[0], angle_column(0, 0), first_rotated[:, 0, :])
        quantise_weight_half(1, 1)
        rotate(first_products[1], angle_column(0, 1), first_rotated[:, 1, :])
        tan, neg_tan = tangents(nc, consts, cos, sin)
        nc.sync.dma_start(out=out_groups[0][0][:, 0:TILES_PER_STORE, :], in_=first_rotated[:])

        steps = {}
        for coming in range(1, GROUPS):
            if coming == 1:
                places = [(0, TILES_PER_STORE + step) for step in range(3)]
            else:
                places = [(coming - 2, 5), (coming - 1, 0), (coming - 1, 1)]
            for step, at in enumerate(places):
                steps[at] = (step, coming)

        for g in range(GROUPS):
            helped = g < HELPED_GROUPS
            for i in range(TILES_PER_STORE if g == 0 else 0, PRODUCTS_PER_GROUP):
                step, coming = steps.get((g, i), (None, None))
                if step == 0:
                    grouped = grouped_pool.tile([P, 4 * GROUP_TOKENS], BF16, align_bytes=64)
                    flipped = [flip_tokens(coming, m) for m in range(2)]
                    regroup(nc.scalar.copy, flipped[0], grouped[:, : 2 * BANK])
                if step == 1:
                    regroup(nc.vector.tensor_copy, flipped[1], grouped[:, 2 * BANK :])
                if step == 2:
                    x_mx[coming] = operand(quantised, "x")
                    quantise(x_mx[coming], 0, grouped[:])

                j, r = divmod(i, TILES_PER_GROUP)
                place = r % TILES_PER_STORE
                if helped and i == (GPSIMD_AT if g else PRODUCTS_PER_GROUP - 2):
                    last_rotated = results.tile([P, TILES_PER_STORE, CHANNELS], F32)
                    last_r = TILES_PER_GROUP - 1
                    rotate_on_gpsimd(
                        project(x_mx[g], w_mx[1], last_r), angle_column(g, last_r), last_rotated[:, 1, :]
                    )
                if helped and i == PRODUCTS_PER_GROUP - 2:
                    rotated = last_rotated
                elif place == 0:
                    rotated = results.tile([P, TILES_PER_STORE, CHANNELS], F32, name="rotated")
                if not (helped and i == PRODUCTS_PER_GROUP - 1):
                    rotate(project(x_mx[g], w_mx[j], r), angle_column(g, r), rotated[:, place, :])
                if place == TILES_PER_STORE - 1:
                    nc.sync.dma_start(out=out_groups[j][g][:, r - place : r + 1, :], in_=rotated[:])
